import numpy as np
import ml_dtypes


def mxq(x, axis, fmt="e4m3"):
    dtype, down = {"e4m3": (ml_dtypes.float8_e4m3fn, 7), "e5m2": (ml_dtypes.float8_e5m2, 14)}[fmt]
    v = np.moveaxis(np.asarray(x, np.float32).astype(ml_dtypes.bfloat16).astype(np.float64), axis, -1)
    blocks = v.reshape(v.shape[:-1] + (-1, 32))
    amax = np.abs(blocks).max(-1, keepdims=True)
    byte = np.maximum(np.where(amax > 0, np.frexp(amax)[1] - 1 + 127, 0) - down, 1)
    scale = np.exp2(byte - 127.0)
    codes = (blocks / scale).astype(np.float32).astype(dtype).astype(np.float64)
    return np.moveaxis((codes * scale).reshape(v.shape), -1, axis)


WIDE = False


def mx_kscale(k):
    if not WIDE:
        return np.ones(k)
    levels = np.array([18, -18])
    if k % 512:
        return np.exp2(np.random.permutation(np.resize(levels, k // 32))).repeat(32)
    a = np.empty((k // 512, 16))
    for p in range(k // 512):
        a[p, :8] = np.random.permutation(np.resize(levels, 8))
        for g in range(8):
            far = levels[np.abs(levels - a[p, g]) >= 10]
            a[p, g + 8] = far[np.random.randint(len(far))]
    return np.exp2(a.ravel()).repeat(32)


BF16 = ml_dtypes.bfloat16


def bf(x):
    return np.asarray(x, np.float32).astype(BF16)


def f64(x):
    return np.asarray(x).astype(np.float64)


B, N, F, U, S = 2, 1024, 256, 256, 2
C = S * (F + U)


def sigmoid(v):
    return 1.0 / (1.0 + np.exp(-v))


def random_walk():
    a = np.random.uniform(size=(N, N))
    return a / a.sum(axis=1, keepdims=True) * np.sqrt(N)


def diffuse(x, sups):
    return np.concatenate([x @ s.T for s in sups], axis=1).transpose(0, 2, 1)


def wide_noise(channels):
    return np.random.standard_normal((B, N, channels)) * np.exp2(np.random.randint(-6, 1, (B, N, 1)))


def setup_inputs():
    u = mx_kscale(2 * U)
    v = mx_kscale(N)
    t = mx_kscale(F + U)
    tc = np.concatenate([t[:F], t[:F], t[F:], t[F:]])
    x0 = bf(np.random.standard_normal((B, F, N)))
    p0 = bf(np.random.standard_normal((B, U, N)))
    s0 = bf(random_walk())
    s1 = bf(random_walk())
    rk = bf(np.random.standard_normal((C, U)) / np.sqrt(C))
    uk = bf(np.random.standard_normal((C, U)) / np.sqrt(C))
    sups = (f64(s0), f64(s1))
    hs = np.concatenate([diffuse(f64(x0), sups), diffuse(f64(p0), sups)], axis=-1)
    r_gate = sigmoid(hs @ f64(rk))
    u_gate = sigmoid(hs @ f64(uk))
    g0 = bf(wide_noise(U) * 4.0 * v[:, None] * u[:U])
    g1 = bf(wide_noise(U) * 4.0 * v[:, None] * u[U:])
    g2 = bf(wide_noise(S * F) * 0.5 * v[:, None] / tc[:S * F])
    return {"inputs": bf(f64(x0) * t[:F, None]).reshape(B, F * N),
            "state": bf(f64(p0) * t[F:, None]).reshape(B, U * N),
            "support0": bf(f64(s0) / v[:, None]),
            "support1": bf(f64(s1) / v[:, None]),
            "r_kernel": bf(f64(rk) / tc[:, None] / u[:U]),
            "u_kernel": bf(f64(uk) / tc[:, None] / u[U:]),
            "r_gate": np.asarray(r_gate, np.float32),
            "u_gate": np.asarray(u_gate, np.float32),
            "grad_0": g0, "grad_1": g1, "grad_2": g2}


def reference(inputs, state, support0, support1, r_kernel, u_kernel, r_gate, u_gate, grad_0, grad_1, grad_2):
    used = S * F + U
    rg = f64(r_gate)
    ug = f64(u_gate)
    dz2 = np.concatenate([f64(grad_0) * rg * (1.0 - rg), f64(grad_1) * ug * (1.0 - ug)], axis=2)
    w2 = np.concatenate([f64(r_kernel)[:used], f64(u_kernel)[:used]], axis=1)
    dhs = mxq(dz2, 2, "e5m2") @ mxq(w2, 1, "e4m3").T
    dh = dhs[:, :, :S * F] + f64(grad_2)
    dst0 = dhs[:, :, S * F:]
    da = dh.reshape(B, N, S, F).transpose(0, 3, 2, 1).reshape(B * F, S * N)
    sup = np.concatenate([f64(support0), f64(support1)], axis=0)
    dx = mxq(da, 1, "e5m2") @ mxq(sup, 0, "e4m3")
    db = np.concatenate([dh[:, :, :F], dst0], axis=2).transpose(1, 0, 2).reshape(N, B * (F + U))
    xs = np.concatenate([f64(inputs).reshape(B, F, N), f64(state).reshape(B, U, N)], axis=1).reshape(B * (F + U), N)
    ds = mxq(db, 1, "e5m2") @ mxq(xs, 0, "e4m3")
    return dx.reshape(B, F * N), ds

@@ -1,0 +1,445 @@
+from contextlib import ExitStack
+
+import concourse.mybir as mybir
+from concourse.masks import make_identity
+
+B, N, F, U = 2, 1024, 256, 256
+
+F32 = mybir.dt.float32
+BF16 = mybir.dt.bfloat16
+U32 = mybir.dt.uint32
+U8 = mybir.dt.uint8
+E4M3 = mybir.dt.float8_e4m3fn_x4
+E5M2 = mybir.dt.float8_e5m2_x4
+ALU = mybir.AluOpType
+
+P = 128
+PACK = 4
+K_PASS = P * PACK
+HALVES = N // K_PASS
+BANK = 512
+WIDE = 2048
+RUN = 4
+Q = P // B
+SUP_COLS = 256
+NB = 4
+NO = 4
+
+FLOPS = 2 * B * N * 512 * 768 + 2 * B * F * 2 * N * N + 2 * N * N * B * (F + U)
+BYTES = 2 * (2 * B * F * N + 2 * N * N + 2 * 768 * U + 2 * B * N * U + B * N * 2 * F) + 4 * (
+    2 * B * N * U + B * F * N + N * N
+)
+
+
+def tile_gcrnncell_pa_v_kernel(
+    tc, inputs, state, support0, support1, r_kernel, u_kernel, r_gate, u_gate, grad_0, grad_1, grad_2, out_0, out_1
+):
+    nc = tc.nc
+    with ExitStack() as ctx:
+        keep = ctx.enter_context(tc.tile_pool(name="keep", bufs=1))
+        work = ctx.enter_context(tc.tile_pool(name="work", bufs=2))
+        psum = ctx.enter_context(tc.psum_pool(name="psum", bufs=8))
+        ctx.enter_context(tc.manual_schedule())
+
+        ident = keep.tile([P, P], F32, name="ident")
+        make_identity(nc, ident[:])
+
+        def bank(name="bank", bufs=NB):
+            return psum.tile([P, BANK], F32, name=name, bufs=bufs)
+
+        def quantise(values, fmt, name):
+            cols = values.shape[1] // PACK
+            codes = keep.tile([P, cols], U32, name=name + "_codes", align_bytes=64)
+            scales = keep.tile([P, cols], U8, name=name + "_scales", align_bytes=64)
+            for c0 in range(0, cols, WIDE // PACK):
+                c1 = min(cols, c0 + WIDE // PACK)
+                nc.vector.quantize_mx(
+                    out=codes[:, c0:c1].bitcast(fmt), scales=scales[:, c0:c1], in_=values[:, PACK * c0 : PACK * c1]
+                )
+            return codes, scales, fmt
+
+        def product(out, lhs, l0, rhs, r0, start, stop):
+            n = out.shape[1]
+            nc.tensor.matmul_mx(
+                out=out,
+                lhsT=lhs[0][:, l0 : l0 + P].bitcast(lhs[2]),
+                lhsT_scale=lhs[1][:, l0 : l0 + P],
+                rhs=rhs[0][:, r0 : r0 + n].bitcast(rhs[2]),
+                rhs_scale=rhs[1][:, r0 : r0 + n],
+                start=start,
+                stop=stop,
+            )
+
+        def copy_on(engine, out, in_):
+            if engine == "vector":
+                nc.vector.tensor_copy(out=out, in_=in_)
+            else:
+                nc.scalar.copy(out=out, in_=in_)
+
+        def interleave(engine, dst, src):
+            copy_on(
+                engine,
+                dst.rearrange("p (c i t) -> p c t i", i=RUN, t=PACK),
+                src.rearrange("p t (c i) -> p c t i", i=RUN),
+            )
+
+        def nodes(x, b, g):
+            return x[b, g * K_PASS : (g + 1) * K_PASS, :].rearrange("(p j) w -> p j w", j=PACK)
+
+        gate_in, g2_in, rows_in = {}, {}, {}
+
+        def load_gate(b, g, s):
+            sig = work.tile([P, PACK, U], F32, name="sig", bufs=4)
+            nc.sync.dma_start(out=sig[:], in_=nodes((r_gate, u_gate)[s], b, g))
+            grad = work.tile([P, PACK, U], BF16, name="grad", bufs=4)
+            nc.sync.dma_start(out=grad[:], in_=nodes((grad_0, grad_1)[s], b, g))
+            gate_in[b, g, s] = (sig, grad)
+
+        def load_grad2(b, g):
+            t = work.tile([P, PACK, 2 * F], BF16, name="grad2", bufs=4)
+            nc.sync.dma_start(out=t[:], in_=nodes(grad_2, b, g))
+            g2_in[b, g] = t
+
+        def load_xs(s, h):
+            t = work.tile([P, PACK, BANK], BF16, name="rows", bufs=8)
+            src = (inputs, state)[s].rearrange("b (q t n) -> (b q) t n", t=PACK, n=N)
+            nc.sync.dma_start(out=t[:], in_=src[:, :, h * BANK : (h + 1) * BANK])
+            rows_in["xs", s, h] = t
+
+        def load_support(i, g, h):
+            t = work.tile([P, PACK, BANK], BF16, name="rows", bufs=8)
+            src = (support0, support1)[i][g * K_PASS : (g + 1) * K_PASS, h * BANK : (h + 1) * BANK]
+            nc.sync.dma_start(out=t[:], in_=src.rearrange("(p j) n -> p j n", j=PACK))
+            rows_in["sup", i, g, h] = t
+
+        def load_w(name, r0, r1):
+            a = (r1 - r0) // P
+            t = keep.tile([P, a, 2, U], BF16, name=name)
+            for s in range(2):
+                nc.sync.dma_start(
+                    out=t[:, :, s, :], in_=(r_kernel, u_kernel)[s][r0:r1, :].rearrange("(p a) k -> p a k", a=a)
+                )
+            return t
+
+        def transpose_w(raw, a0):
+            words = raw[:].rearrange("p a s k -> p (a s k)").bitcast(F32)
+            t = bank()
+            for a in range(2):
+                for u in range(2):
+                    w0 = (a0 + a) * 2 * P
+                    c0 = (2 * a + u) * P
+                    nc.tensor.transpose(t[:, c0 : c0 + P], words[:, w0 + u : w0 + 2 * P : 2], ident[:])
+            return t
+
+        def turn_w_main(w_main):
+            wt = work.tile([P, WIDE], BF16, name="stage", bufs=8, align_bytes=64)
+            dst = wt[:].bitcast(F32).rearrange("k (p a u) -> k p a u", a=PACK, u=2)
+            for a0 in (0, 2):
+                t = transpose_w(w_main, a0)
+                nc.scalar.copy(out=dst[:, :, a0 : a0 + 2, :], in_=t[:].rearrange("k (a u p) -> k p a u", a=2, u=2))
+            return wt[:]
+
+        def turn_w_unit(w_unit):
+            wu = keep.tile([P, 2 * PACK + 1, Q * PACK], BF16, name="w_unit_padded", align_bytes=64)
+            nc.gpsimd.memset(wu[:, 0 : 2 * PACK + 1 : 2, :], 0.0)
+            t = transpose_w(w_unit, 0)
+            wu_flat = wu[:].rearrange("k s c -> k (s c)")
+            sections = wu_flat.bitcast(F32)[:, 2 * Q :].rearrange("k (h a z q u) -> k h a z q u", h=2, a=2, z=2, u=2)
+            nc.scalar.copy(
+                out=sections[:, :, :, 0, :, :], in_=t[:].rearrange("k (a u q h) -> k h a q u", a=2, u=2, h=2)
+            )
+            return wu_flat
+
+        dz_rows, dz_q, dh_vals, dh_q, db_q = {}, {}, {}, {}, {}
+
+        def gate_grad(b, g, s):
+            sig, grad = gate_in[b, g, s]
+            if s == 0:
+                dz_rows[b, g] = work.tile([P, PACK, 2, 2, P], BF16, name="dz_rows", bufs=2)
+            part = work.tile([P, PACK, U], F32, name="part", bufs=2)
+            nc.vector.scalar_tensor_tensor(
+                out=part[:], in0=sig[:], scalar=1.0, in1=grad[:], op0=ALU.subtract, op1=ALU.mult
+            )
+            return part
+
+        def gate_round(b, g, s, part):
+            sig = gate_in[b, g, s][0]
+            for u in range(2):
+                nc.vector.scalar_tensor_tensor(
+                    out=dz_rows[b, g][:, :, u, s, :].rearrange("p j (w e) -> p j w e", e=2),
+                    in0=part[:].rearrange("p j (w u e) -> p j w u e", u=2, e=2)[:, :, :, u, :],
+                    scalar=-1.0,
+                    in1=sig[:].rearrange("p j (w u e) -> p j w u e", u=2, e=2)[:, :, :, u, :],
+                    op0=ALU.mult,
+                    op1=ALU.mult,
+                )
+
+        def gate(b, g, s):
+            gate_round(b, g, s, gate_grad(b, g, s))
+
+        def turn_dz(b, g):
+            words = dz_rows[b, g][:].rearrange("p j u s w -> p (j u s w)").bitcast(F32)
+            zt = work.tile([P, WIDE], BF16, name="stage", bufs=8, align_bytes=64)
+            for h in range(2):
+                t = bank()
+                for c in range(PACK):
+                    w0 = (PACK * h + c) * P
+                    nc.tensor.transpose(t[:, c * P : (c + 1) * P], words[:, w0 : w0 + P], ident[:])
+                nc.scalar.copy(
+                    out=zt[:].bitcast(F32)[:, h * BANK : (h + 1) * BANK].rearrange("k (j p u) -> k j p u", j=2, u=2),
+                    in_=t[:].rearrange("k (j u p) -> k j p u", j=2, u=2),
+                )
+            return zt
+
+        def quantise_dz(b, g, zt):
+            dz_q[b, g] = quantise(zt[:], E5M2, "dz_%d_%d" % (b, g))
+
+        def dh_part(b, g, i, w_main_q):
+            if b == 0:
+                dh_vals[g, i] = work.tile([P, B, F * PACK], BF16, name="dh_vals", bufs=4, align_bytes=64)
+            for h in range(2):
+                c0 = i * F + h * P
+                t = bank()
+                for j in range(PACK):
+                    product(t[:, j * P : (j + 1) * P], dz_q[b, g], j * P, w_main_q, c0, True, True)
+                nc.vector.tensor_tensor(
+                    out=dh_vals[g, i][:, b, h * BANK : (h + 1) * BANK].rearrange(
+                        "p (c r j) -> p c j r", r=RUN, j=PACK
+                    ),
+                    in0=t[:].rearrange("p (j c r) -> p c j r", j=PACK, r=RUN),
+                    in1=g2_in[b, g][:, :, c0 : c0 + P].rearrange("p j (c r) -> p c j r", r=RUN),
+                    op=ALU.add,
+                )
+
+        def quantise_dh(g, i):
+            dh_q[g, i] = quantise(dh_vals[g, i][:].rearrange("p b c -> p (b c)"), E5M2, "dh_%d_%d" % (g, i))
+
+        def turn_dh0(g):
+            words = dh_vals[g, 0][:].rearrange("p b c -> p (b c)").bitcast(F32)
+            vals = work.tile([P, WIDE], BF16, name="stage", bufs=8, align_bytes=64)
+            for u in range(2):
+                t = bank()
+                for c in range(PACK):
+                    nc.tensor.transpose(t[:, c * P : (c + 1) * P], words[:, 2 * c + u : 2 * BANK : 2 * PACK], ident[:])
+                nc.scalar.copy(
+                    out=vals[:, u * 2 * BANK : (u + 1) * 2 * BANK].rearrange("k (e p c) -> k e p c", e=2, c=PACK),
+                    in_=t[:].bitcast(BF16).rearrange("k (c p e) -> k e p c", c=PACK, e=2),
+                )
+            return vals
+
+        def dst_part(g, w_unit_q):
+            vals = work.tile([P, WIDE], BF16, name="stage", bufs=8, align_bytes=64)
+            for j in range(PACK):
+                t = bank()
+                for c in range(PACK):
+                    for b in range(B):
+                        product(
+                            t[:, c * P : (c + 1) * P], w_unit_q, (2 * c + 1 - b) * Q, dz_q[b, g], j * P, b == 0, b == 1
+                        )
+                nc.scalar.copy(
+                    out=vals[:, j * BANK : (j + 1) * BANK].rearrange("k (p c) -> k p c", c=PACK),
+                    in_=t[:].rearrange("k (c p) -> k p c", c=PACK),
+                )
+            return vals
+
+        def quantise_db(g, s, vals):
+            db_q[g, s] = quantise(vals[:], E5M2, "db_%d_%d" % (g, s))
+
+        xs_q, sup_q = {}, {}
+
+        def stage():
+            return work.tile([P, WIDE], BF16, name="stage", bufs=8, align_bytes=64)
+
+        def xs_weave(vals, s, h, c, engine):
+            interleave(engine, vals[:, c * 1024 : (c + 1) * 1024], rows_in["xs", s, h][:, :, c * 256 : (c + 1) * 256])
+
+        def quantise_xs(s, h, vals):
+            xs_q[s, h] = quantise(vals[:], E4M3, "xs_%d_%d" % (s, h))
+
+        def sup_weave(vals, i, quarter, g, engine):
+            c0 = quarter % 2 * SUP_COLS
+            interleave(
+                engine, vals[:, g * 1024 : (g + 1) * 1024], rows_in["sup", i, g, quarter // 2][:, :, c0 : c0 + SUP_COLS]
+            )
+
+        def quantise_sup(i, quarter, vals):
+            sup_q[i, quarter] = quantise(vals[:], E4M3, "sup_%d_%d" % (i, quarter))
+
+        out_1_rows = out_1.rearrange("(g p j) n -> g j p n", p=P, j=PACK)
+        out_0_rows = out_0.rearrange("b (h p n) -> p (b h) n", p=P, n=N)
+
+        def out_1_part(g, j, engines):
+            res = work.tile([P, N], F32, name="res", bufs=6)
+            for h in range(2):
+                t = bank("out", NO)
+                for s in range(2):
+                    product(t[:], db_q[g, s], j * P, xs_q[s, h], 0, s == 0, s == 1)
+                copy_on(engines[h], res[:, h * BANK : (h + 1) * BANK], t[:])
+            nc.sync.dma_start(out=out_1_rows[g, j], in_=res[:])
+
+        def out_0_passes(t, cols, s, quarter, i):
+            for g in range(HALVES):
+                product(
+                    t[:, cols], dh_q[g, i], s * P, sup_q[i, quarter], g * SUP_COLS, i + g == 0, i + g == HALVES
+                )
+
+        def out_0_store(res, quarter, s0, s1):
+            nc.sync.dma_start(
+                out=out_0_rows[:, s0:s1, quarter * SUP_COLS : (quarter + 1) * SUP_COLS],
+                in_=res[:, s0 * SUP_COLS : s1 * SUP_COLS].rearrange("p (s n) -> p s n", n=SUP_COLS),
+            )
+
+        def out_0_part(quarter, engines):
+            res = work.tile([P, N], F32, name="res", bufs=6)
+            for b in range(B):
+                t = bank("out", NO)
+                for h in range(2):
+                    for i in range(2):
+                        out_0_passes(t, slice(h * SUP_COLS, (h + 1) * SUP_COLS), 2 * b + h, quarter, i)
+                copy_on(engines[b], res[:, b * BANK : (b + 1) * BANK], t[:])
+            out_0_store(res, quarter, 0, PACK)
+
+        def out_0_open(quarter):
+            banks = [bank("out", NO) for s in range(PACK)]
+            for s in range(PACK):
+                out_0_passes(banks[s], slice(0, SUP_COLS), s, quarter, 0)
+            return banks
+
+        def out_0_close(quarter, banks):
+            res = work.tile([P, N], F32, name="res", bufs=6)
+            for s in range(PACK):
+                out_0_passes(banks[s], slice(0, SUP_COLS), s, quarter, 1)
+                copy_on(("scalar", "vector")[s % 2], res[:, s * SUP_COLS : (s + 1) * SUP_COLS], banks[s][:, :SUP_COLS])
+                if s % 2:
+                    out_0_store(res, quarter, s - 1, s + 1)
+
+        S, V = "scalar", "vector"
+        load_gate(0, 0, 0)
+        load_xs(0, 0)
+        load_gate(0, 0, 1)
+        w_main = load_w("w_main_rows", 0, 2 * F)
+        load_gate(1, 0, 0)
+        load_xs(0, 1)
+        load_grad2(0, 0)
+        load_gate(1, 0, 1)
+        w_unit = load_w("w_unit_rows", 2 * F, 2 * F + U)
+        load_xs(1, 0)
+
+        x00, x01 = stage(), stage()
+        gate(0, 0, 0)
+        load_gate(0, 1, 0)
+        load_grad2(1, 0)
+        load_xs(1, 1)
+        xs_weave(x00, 0, 0, 0, S)
+        xs_weave(x00, 0, 0, 1, S)
+        part = gate_grad(0, 0, 1)
+        quantise_xs(0, 0, x00)
+        gate_round(0, 0, 1, part)
+        load_gate(0, 1, 1)
+        wt = turn_w_main(w_main)
+        zt = turn_dz(0, 0)
+        xs_weave(x01, 0, 1, 0, S)
+        xs_weave(x01, 0, 1, 1, S)
+        part = gate_grad(1, 0, 0)
+        w_main_q = quantise(wt, E4M3, "w_main")
+        gate_round(1, 0, 0, part)
+        load_gate(1, 1, 0)
+        load_support(0, 0, 0)
+        quantise_dz(0, 0, zt)
+        part = gate_grad(1, 0, 1)
+        dh_part(0, 0, 0, w_main_q)
+        gate_round(1, 0, 1, part)
+        load_gate(1, 1, 1)
+        load_support(0, 1, 0)
+        load_grad2(0, 1)
+        load_grad2(1, 1)
+        load_support(1, 0, 0)
+        load_support(1, 1, 0)
+        wu = turn_w_unit(w_unit)
+        x10 = stage()
+        xs_weave(x10, 1, 0, 0, S)
+        xs_weave(x10, 1, 0, 1, S)
+        zt = turn_dz(1, 0)
+        w_unit_q = quantise(wu, E4M3, "w_unit")
+        part = gate_grad(0, 1, 0)
+        quantise_dz(1, 0, zt)
+        gate_round(0, 1, 0, part)
+        dh_part(1, 0, 0, w_main_q)
+        x11 = stage()
+        xs_weave(x11, 1, 1, 0, S)
+        dst = dst_part(0, w_unit_q)
+        xs_weave(x11, 1, 1, 1, S)
+        for i in range(2):
+            for g in range(2):
+                load_support(i, g, 1)
+        dht = turn_dh0(0)
+        quantise_xs(0, 1, x01)
+        part = gate_grad(0, 1, 1)
+        quantise_xs(1, 0, x10)
+        gate_round(0, 1, 1, part)
+        zt = turn_dz(0, 1)
+        quantise_db(0, 1, dst)
+        part = gate_grad(1, 1, 0)
+        quantise_xs(1, 1, x11)
+        quantise_db(0, 0, dht)
+        gate_round(1, 1, 0, part)
+        s00, s10 = stage(), stage()
+        sup_weave(s00, 0, 0, 0, S)
+        out_1_part(0, 0, (S, S))
+        part = gate_grad(1, 1, 1)
+        quantise_dz(0, 1, zt)
+        gate_round(1, 1, 1, part)
+        out_1_part(0, 1, (S, S))
+        dh_part(0, 1, 0, w_main_q)
+        zt = turn_dz(1, 1)
+        out_1_part(0, 2, (S, S))
+        quantise_dh(0, 0)
+        s01, s11 = stage(), stage()
+        sup_weave(s11, 1, 1, 0, V)
+        quantise_dz(1, 1, zt)
+        sup_weave(s11, 1, 1, 1, V)
+        out_1_part(0, 3, (S, S))
+        dh_part(1, 1, 0, w_main_q)
+        sup_weave(s00, 0, 0, 1, S)
+        dst = dst_part(1, w_unit_q)
+        dht = turn_dh0(1)
+        quantise_sup(1, 1, s11)
+        quantise_dh(1, 0)
+        quantise_sup(0, 0, s00)
+        s02 = stage()
+        sup_weave(s02, 0, 2, 0, V)
+        sup_weave(s02, 0, 2, 1, V)
+        quantise_db(1, 1, dst)
+        quantise_sup(0, 2, s02)
+        dh_part(0, 0, 1, w_main_q)
+        quantise_db(1, 0, dht)
+        sup_weave(s10, 1, 0, 0, S)
+        sup_weave(s10, 1, 0, 1, S)
+        dh_part(1, 0, 1, w_main_q)
+        dh_part(0, 1, 1, w_main_q)
+        out_1_part(1, 0, (S, S))
+        dh_part(1, 1, 1, w_main_q)
+        out_1_part(1, 1, (S, S))
+        out_1_part(1, 2, (S, S))
+        out_1_part(1, 3, (S, S))
+        quantise_dh(0, 1)
+        quantise_sup(1, 0, s10)
+        quantise_dh(1, 1)
+        sup_weave(s01, 0, 1, 0, S)
+        sup_weave(s01, 0, 1, 1, V)
+        out_0_part(0, (S, S))
+        s12 = stage()
+        sup_weave(s12, 1, 2, 0, V)
+        quantise_sup(0, 1, s01)
+        sup_weave(s12, 1, 2, 1, S)
+        out_0_part(1, (S, S))
+        s03, s13 = stage(), stage()
+        sup_weave(s03, 0, 3, 0, V)
+        sup_weave(s03, 0, 3, 1, V)
+        quantise_sup(1, 2, s12)
+        sup_weave(s13, 1, 3, 1, S)
+        sup_weave(s13, 1, 3, 0, V)
+        quantise_sup(0, 3, s03)
+        out_0_part(2, (S, S))
+        quantise_sup(1, 3, s13)
+        out_0_close(3, out_0_open(3))

@@ -22,7 +22,7 @@ WIDE = 2048
 RUN = 4
 Q = P // B
 SUP_COLS = 256
-NB = 4
+NB = 8
 NO = 4
 
 FLOPS = 2 * B * N * 512 * 768 + 2 * B * F * 2 * N * N + 2 * N * N * B * (F + U)
@@ -100,17 +100,16 @@ def tile_gcrnncell_pa_v_kernel(
             nc.sync.dma_start(out=t[:], in_=nodes(grad_2, b, g))
             g2_in[b, g] = t
 
-        def load_xs(s, h):
-            t = work.tile([P, PACK, BANK], BF16, name="rows", bufs=8)
-            src = (inputs, state)[s].rearrange("b (q t n) -> (b q) t n", t=PACK, n=N)
-            nc.sync.dma_start(out=t[:], in_=src[:, :, h * BANK : (h + 1) * BANK])
-            rows_in["xs", s, h] = t
+        def load_xs(s):
+            t = work.tile([P, PACK, N], BF16, name="rows", bufs=4)
+            nc.sync.dma_start(out=t[:], in_=(inputs, state)[s].rearrange("b (q t n) -> (b q) t n", t=PACK, n=N))
+            rows_in["xs", s] = t
 
-        def load_support(i, g, h):
-            t = work.tile([P, PACK, BANK], BF16, name="rows", bufs=8)
-            src = (support0, support1)[i][g * K_PASS : (g + 1) * K_PASS, h * BANK : (h + 1) * BANK]
+        def load_support(i, g):
+            t = work.tile([P, PACK, N], BF16, name="rows", bufs=4)
+            src = (support0, support1)[i][g * K_PASS : (g + 1) * K_PASS, :]
             nc.sync.dma_start(out=t[:], in_=src.rearrange("(p j) n -> p j n", j=PACK))
-            rows_in["sup", i, g, h] = t
+            rows_in["sup", i, g] = t
 
         def load_w(name, r0, r1):
             a = (r1 - r0) // P
@@ -132,7 +131,7 @@ def tile_gcrnncell_pa_v_kernel(
             return t
 
         def turn_w_main(w_main):
-            wt = work.tile([P, WIDE], BF16, name="stage", bufs=8, align_bytes=64)
+            wt = work.tile([P, WIDE], BF16, name="stage", bufs=9, align_bytes=64)
             dst = wt[:].bitcast(F32).rearrange("k (p a u) -> k p a u", a=PACK, u=2)
             for a0 in (0, 2):
                 t = transpose_w(w_main, a0)
@@ -150,7 +149,7 @@ def tile_gcrnncell_pa_v_kernel(
             )
             return wu_flat
 
-        dz_rows, dz_q, dh_vals, dh_q, db_q = {}, {}, {}, {}, {}
+        dz_rows, dz_q, dh_banks, dh_vals, dh_q, db_q = {}, {}, {}, {}, {}, {}
 
         def gate_grad(b, g, s):
             sig, grad = gate_in[b, g, s]
@@ -179,7 +178,7 @@ def tile_gcrnncell_pa_v_kernel(
 
         def turn_dz(b, g):
             words = dz_rows[b, g][:].rearrange("p j u s w -> p (j u s w)").bitcast(F32)
-            zt = work.tile([P, WIDE], BF16, name="stage", bufs=8, align_bytes=64)
+            zt = work.tile([P, WIDE], BF16, name="stage", bufs=9, align_bytes=64)
             for h in range(2):
                 t = bank()
                 for c in range(PACK):
@@ -194,33 +193,35 @@ def tile_gcrnncell_pa_v_kernel(
         def quantise_dz(b, g, zt):
             dz_q[b, g] = quantise(zt[:], E5M2, "dz_%d_%d" % (b, g))
 
-        def dh_part(b, g, i, w_main_q):
+        def dh_products(b, g, i, w_main_q):
+            banks = [bank(), bank()]
+            for h in range(2):
+                for j in range(PACK):
+                    product(banks[h][:, j * P : (j + 1) * P], dz_q[b, g], j * P, w_main_q, i * F + h * P, True, True)
+            dh_banks[b, g, i] = banks
+
+        def dh_add(b, g, i):
             if b == 0:
-                dh_vals[g, i] = work.tile([P, B, F * PACK], BF16, name="dh_vals", bufs=4, align_bytes=64)
+                dh_vals[g, i] = work.tile([P, PACK, B, Q, PACK], BF16, name="dh_vals", bufs=4, align_bytes=64)
             for h in range(2):
                 c0 = i * F + h * P
-                t = bank()
-                for j in range(PACK):
-                    product(t[:, j * P : (j + 1) * P], dz_q[b, g], j * P, w_main_q, c0, True, True)
                 nc.vector.tensor_tensor(
-                    out=dh_vals[g, i][:, b, h * BANK : (h + 1) * BANK].rearrange(
-                        "p (c r j) -> p c j r", r=RUN, j=PACK
-                    ),
-                    in0=t[:].rearrange("p (j c r) -> p c j r", j=PACK, r=RUN),
-                    in1=g2_in[b, g][:, :, c0 : c0 + P].rearrange("p j (c r) -> p c j r", r=RUN),
+                    out=dh_vals[g, i][:, :, b, h * Q // 2 : (h + 1) * Q // 2, :].rearrange("p r c j -> p c j r"),
+                    in0=dh_banks[b, g, i][h][:].rearrange("p (j c r) -> p c j r", j=PACK, r=PACK),
+                    in1=g2_in[b, g][:, :, c0 : c0 + P].rearrange("p j (c r) -> p c j r", r=PACK),
                     op=ALU.add,
                 )
 
         def quantise_dh(g, i):
-            dh_q[g, i] = quantise(dh_vals[g, i][:].rearrange("p b c -> p (b c)"), E5M2, "dh_%d_%d" % (g, i))
+            dh_q[g, i] = quantise(dh_vals[g, i][:].rearrange("p r b q j -> p (r b q j)"), E5M2, "dh_%d_%d" % (g, i))
 
         def turn_dh0(g):
-            words = dh_vals[g, 0][:].rearrange("p b c -> p (b c)").bitcast(F32)
-            vals = work.tile([P, WIDE], BF16, name="stage", bufs=8, align_bytes=64)
+            words = dh_vals[g, 0][:].rearrange("p r b q j -> p (r b q j)").bitcast(F32)
+            vals = work.tile([P, WIDE], BF16, name="stage", bufs=9, align_bytes=64)
             for u in range(2):
                 t = bank()
                 for c in range(PACK):
-                    nc.tensor.transpose(t[:, c * P : (c + 1) * P], words[:, 2 * c + u : 2 * BANK : 2 * PACK], ident[:])
+                    nc.tensor.transpose(t[:, c * P : (c + 1) * P], words[:, 2 * c * P + u : 2 * (c + 1) * P : 2], ident[:])
                 nc.scalar.copy(
                     out=vals[:, u * 2 * BANK : (u + 1) * 2 * BANK].rearrange("k (e p c) -> k e p c", e=2, c=PACK),
                     in_=t[:].bitcast(BF16).rearrange("k (c p e) -> k e p c", c=PACK, e=2),
@@ -228,7 +229,7 @@ def tile_gcrnncell_pa_v_kernel(
             return vals
 
         def dst_part(g, w_unit_q):
-            vals = work.tile([P, WIDE], BF16, name="stage", bufs=8, align_bytes=64)
+            vals = work.tile([P, WIDE], BF16, name="stage", bufs=9, align_bytes=64)
             for j in range(PACK):
                 t = bank()
                 for c in range(PACK):
@@ -248,30 +249,30 @@ def tile_gcrnncell_pa_v_kernel(
         xs_q, sup_q = {}, {}
 
         def stage():
-            return work.tile([P, WIDE], BF16, name="stage", bufs=8, align_bytes=64)
+            return work.tile([P, WIDE], BF16, name="stage", bufs=9, align_bytes=64)
 
         def xs_weave(vals, s, h, c, engine):
-            interleave(engine, vals[:, c * 1024 : (c + 1) * 1024], rows_in["xs", s, h][:, :, c * 256 : (c + 1) * 256])
+            interleave(engine, vals[:, c * 1024 : (c + 1) * 1024], rows_in["xs", s][:, :, (2 * h + c) * 256 : (2 * h + c + 1) * 256])
 
         def quantise_xs(s, h, vals):
             xs_q[s, h] = quantise(vals[:], E4M3, "xs_%d_%d" % (s, h))
 
         def sup_weave(vals, i, quarter, g, engine):
-            c0 = quarter % 2 * SUP_COLS
+            c0 = quarter * SUP_COLS
             interleave(
-                engine, vals[:, g * 1024 : (g + 1) * 1024], rows_in["sup", i, g, quarter // 2][:, :, c0 : c0 + SUP_COLS]
+                engine, vals[:, g * 1024 : (g + 1) * 1024], rows_in["sup", i, g][:, :, c0 : c0 + SUP_COLS]
             )
 
         def quantise_sup(i, quarter, vals):
             sup_q[i, quarter] = quantise(vals[:], E4M3, "sup_%d_%d" % (i, quarter))
 
         out_1_rows = out_1.rearrange("(g p j) n -> g j p n", p=P, j=PACK)
-        out_0_rows = out_0.rearrange("b (h p n) -> p (b h) n", p=P, n=N)
+        out_0_rows = out_0.rearrange("b (q r n) -> (b q) r n", r=PACK, n=N)
 
         def out_1_part(g, j, engines):
-            res = work.tile([P, N], F32, name="res", bufs=6)
+            res = work.tile([P, N], F32, name="res", bufs=5)
             for h in range(2):
-                t = bank("out", NO)
+                t = bank()
                 for s in range(2):
                     product(t[:], db_q[g, s], j * P, xs_q[s, h], 0, s == 0, s == 1)
                 copy_on(engines[h], res[:, h * BANK : (h + 1) * BANK], t[:])
@@ -290,9 +291,9 @@ def tile_gcrnncell_pa_v_kernel(
             )
 
         def out_0_part(quarter, engines):
-            res = work.tile([P, N], F32, name="res", bufs=6)
+            res = work.tile([P, N], F32, name="res", bufs=5)
             for b in range(B):
-                t = bank("out", NO)
+                t = bank()
                 for h in range(2):
                     for i in range(2):
                         out_0_passes(t, slice(h * SUP_COLS, (h + 1) * SUP_COLS), 2 * b + h, quarter, i)
@@ -300,13 +301,13 @@ def tile_gcrnncell_pa_v_kernel(
             out_0_store(res, quarter, 0, PACK)
 
         def out_0_open(quarter):
-            banks = [bank("out", NO) for s in range(PACK)]
+            banks = [bank() for s in range(PACK)]
             for s in range(PACK):
                 out_0_passes(banks[s], slice(0, SUP_COLS), s, quarter, 0)
             return banks
 
         def out_0_close(quarter, banks):
-            res = work.tile([P, N], F32, name="res", bufs=6)
+            res = work.tile([P, N], F32, name="res", bufs=5)
             for s in range(PACK):
                 out_0_passes(banks[s], slice(0, SUP_COLS), s, quarter, 1)
                 copy_on(("scalar", "vector")[s % 2], res[:, s * SUP_COLS : (s + 1) * SUP_COLS], banks[s][:, :SUP_COLS])
@@ -315,131 +316,139 @@ def tile_gcrnncell_pa_v_kernel(
 
         S, V = "scalar", "vector"
         load_gate(0, 0, 0)
-        load_xs(0, 0)
         load_gate(0, 0, 1)
-        w_main = load_w("w_main_rows", 0, 2 * F)
         load_gate(1, 0, 0)
-        load_xs(0, 1)
-        load_grad2(0, 0)
+        w_main = load_w("w_main_rows", 0, 2 * F)
         load_gate(1, 0, 1)
-        w_unit = load_w("w_unit_rows", 2 * F, 2 * F + U)
-        load_xs(1, 0)
-
-        x00, x01 = stage(), stage()
-        gate(0, 0, 0)
+        load_xs(0)
+        part_000 = gate_grad(0, 0, 0)
+        gate_round(0, 0, 0, part_000)
         load_gate(0, 1, 0)
+        w_unit = load_w("w_unit_rows", 2 * F, 2 * F + U)
+        load_grad2(0, 0)
+        load_xs(1)
         load_grad2(1, 0)
-        load_xs(1, 1)
-        xs_weave(x00, 0, 0, 0, S)
-        xs_weave(x00, 0, 0, 1, S)
-        part = gate_grad(0, 0, 1)
-        quantise_xs(0, 0, x00)
-        gate_round(0, 0, 1, part)
+        part_001 = gate_grad(0, 0, 1)
+        part_100 = gate_grad(1, 0, 0)
+        gate_round(0, 0, 1, part_001)
         load_gate(0, 1, 1)
         wt = turn_w_main(w_main)
-        zt = turn_dz(0, 0)
-        xs_weave(x01, 0, 1, 0, S)
-        xs_weave(x01, 0, 1, 1, S)
-        part = gate_grad(1, 0, 0)
-        w_main_q = quantise(wt, E4M3, "w_main")
-        gate_round(1, 0, 0, part)
+        z00 = turn_dz(0, 0)
+        gate_round(1, 0, 0, part_100)
         load_gate(1, 1, 0)
-        load_support(0, 0, 0)
-        quantise_dz(0, 0, zt)
-        part = gate_grad(1, 0, 1)
-        dh_part(0, 0, 0, w_main_q)
-        gate_round(1, 0, 1, part)
+        part_101 = gate_grad(1, 0, 1)
+        w_main_q = quantise(wt, E4M3, "w_main")
+        gate_round(1, 0, 1, part_101)
+        load_support(0, 0)
         load_gate(1, 1, 1)
-        load_support(0, 1, 0)
         load_grad2(0, 1)
+        load_support(0, 1)
         load_grad2(1, 1)
-        load_support(1, 0, 0)
-        load_support(1, 1, 0)
+        quantise_dz(0, 0, z00)
+        x00 = stage()
+        xs_weave(x00, 0, 0, 0, S)
+        x01 = stage()
+        xs_weave(x01, 0, 1, 0, V)
+        z10 = turn_dz(1, 0)
+        xs_weave(x00, 0, 0, 1, S)
         wu = turn_w_unit(w_unit)
+        xs_weave(x01, 0, 1, 1, S)
+        load_support(1, 0)
+        part_010 = gate_grad(0, 1, 0)
+        quantise_dz(1, 0, z10)
+        gate_round(0, 1, 0, part_010)
+        w_unit_q = quantise(wu, E4M3, "w_unit")
+        dh_products(0, 0, 0, w_main_q)
+        dh_products(1, 0, 0, w_main_q)
+        dh_add(0, 0, 0)
+        dh_add(1, 0, 0)
         x10 = stage()
         xs_weave(x10, 1, 0, 0, S)
+        d0 = dst_part(0, w_unit_q)
         xs_weave(x10, 1, 0, 1, S)
-        zt = turn_dz(1, 0)
-        w_unit_q = quantise(wu, E4M3, "w_unit")
-        part = gate_grad(0, 1, 0)
-        quantise_dz(1, 0, zt)
-        gate_round(0, 1, 0, part)
-        dh_part(1, 0, 0, w_main_q)
+        t0 = turn_dh0(0)
         x11 = stage()
-        xs_weave(x11, 1, 1, 0, S)
-        dst = dst_part(0, w_unit_q)
-        xs_weave(x11, 1, 1, 1, S)
-        for i in range(2):
-            for g in range(2):
-                load_support(i, g, 1)
-        dht = turn_dh0(0)
+        xs_weave(x11, 1, 1, 0, V)
+        part_011 = gate_grad(0, 1, 1)
+        quantise_xs(0, 0, x00)
+        gate_round(0, 1, 1, part_011)
         quantise_xs(0, 1, x01)
-        part = gate_grad(0, 1, 1)
-        quantise_xs(1, 0, x10)
-        gate_round(0, 1, 1, part)
-        zt = turn_dz(0, 1)
-        quantise_db(0, 1, dst)
-        part = gate_grad(1, 1, 0)
-        quantise_xs(1, 1, x11)
-        quantise_db(0, 0, dht)
-        gate_round(1, 1, 0, part)
-        s00, s10 = stage(), stage()
+        xs_weave(x11, 1, 1, 1, S)
+        z01 = turn_dz(0, 1)
+        load_support(1, 1)
+        s00 = stage()
         sup_weave(s00, 0, 0, 0, S)
+        s01 = stage()
+        sup_weave(s01, 0, 1, 0, S)
+        quantise_db(0, 1, d0)
+        part_110 = gate_grad(1, 1, 0)
+        quantise_xs(1, 0, x10)
+        quantise_db(0, 0, t0)
+        quantise_xs(1, 1, x11)
+        gate_round(1, 1, 0, part_110)
+        quantise_dz(0, 1, z01)
         out_1_part(0, 0, (S, S))
-        part = gate_grad(1, 1, 1)
-        quantise_dz(0, 1, zt)
-        gate_round(1, 1, 1, part)
         out_1_part(0, 1, (S, S))
-        dh_part(0, 1, 0, w_main_q)
-        zt = turn_dz(1, 1)
+        dh_products(0, 1, 0, w_main_q)
+        dh_products(0, 0, 1, w_main_q)
+        part_111 = gate_grad(1, 1, 1)
+        s02 = stage()
+        sup_weave(s02, 0, 2, 0, S)
+        gate_round(1, 1, 1, part_111)
+        z11 = turn_dz(1, 1)
+        dh_add(0, 1, 0)
+        dh_products(1, 0, 1, w_main_q)
+        dh_add(0, 0, 1)
         out_1_part(0, 2, (S, S))
-        quantise_dh(0, 0)
-        s01, s11 = stage(), stage()
-        sup_weave(s11, 1, 1, 0, V)
-        quantise_dz(1, 1, zt)
-        sup_weave(s11, 1, 1, 1, V)
-        out_1_part(0, 3, (S, S))
-        dh_part(1, 1, 0, w_main_q)
+        quantise_dz(1, 1, z11)
+        dh_products(1, 1, 0, w_main_q)
+        dh_add(1, 0, 1)
+        dh_add(1, 1, 0)
         sup_weave(s00, 0, 0, 1, S)
-        dst = dst_part(1, w_unit_q)
-        dht = turn_dh0(1)
-        quantise_sup(1, 1, s11)
+        d1 = dst_part(1, w_unit_q)
+        t1 = turn_dh0(1)
+        dh_products(0, 1, 1, w_main_q)
+        dh_products(1, 1, 1, w_main_q)
+        quantise_dh(0, 0)
+        quantise_dh(0, 1)
         quantise_dh(1, 0)
         quantise_sup(0, 0, s00)
-        s02 = stage()
-        sup_weave(s02, 0, 2, 0, V)
-        sup_weave(s02, 0, 2, 1, V)
-        quantise_db(1, 1, dst)
-        quantise_sup(0, 2, s02)
-        dh_part(0, 0, 1, w_main_q)
-        quantise_db(1, 0, dht)
-        sup_weave(s10, 1, 0, 0, S)
+        quantise_db(1, 1, d1)
+        dh_add(0, 1, 1)
+        quantise_db(1, 0, t1)
+        dh_add(1, 1, 1)
+        out_1_part(0, 3, (S, S))
+        s10 = stage()
+        sup_weave(s10, 1, 0, 0, V)
         sup_weave(s10, 1, 0, 1, S)
-        dh_part(1, 0, 1, w_main_q)
-        dh_part(0, 1, 1, w_main_q)
         out_1_part(1, 0, (S, S))
-        dh_part(1, 1, 1, w_main_q)
         out_1_part(1, 1, (S, S))
+        quantise_dh(1, 1)
+        quantise_sup(1, 0, s10)
+        sup_weave(s01, 0, 1, 1, V)
+        s11 = stage()
+        sup_weave(s11, 1, 1, 0, V)
         out_1_part(1, 2, (S, S))
         out_1_part(1, 3, (S, S))
-        quantise_dh(0, 1)
-        quantise_sup(1, 0, s10)
-        quantise_dh(1, 1)
-        sup_weave(s01, 0, 1, 0, S)
-        sup_weave(s01, 0, 1, 1, V)
-        out_0_part(0, (S, S))
+        sup_weave(s11, 1, 1, 1, V)
+        quantise_sup(0, 1, s01)
+        sup_weave(s02, 0, 2, 1, V)
+        quantise_sup(1, 1, s11)
         s12 = stage()
         sup_weave(s12, 1, 2, 0, V)
-        quantise_sup(0, 1, s01)
+        out_0_part(0, (S, S))
         sup_weave(s12, 1, 2, 1, S)
-        out_0_part(1, (S, S))
-        s03, s13 = stage(), stage()
+        quantise_sup(0, 2, s02)
+        s03 = stage()
         sup_weave(s03, 0, 3, 0, V)
-        sup_weave(s03, 0, 3, 1, V)
         quantise_sup(1, 2, s12)
-        sup_weave(s13, 1, 3, 1, S)
-        sup_weave(s13, 1, 3, 0, V)
+        sup_weave(s03, 0, 3, 1, V)
+        out_0_part(1, (S, S))
+        s13 = stage()
+        sup_weave(s13, 1, 3, 0, S)
         quantise_sup(0, 3, s03)
+        sup_weave(s13, 1, 3, 1, V)
         out_0_part(2, (S, S))
         quantise_sup(1, 3, s13)
-        out_0_close(3, out_0_open(3))
+        last = out_0_open(3)
+        out_0_close(3, last)

@@ -23,7 +23,7 @@ RUN = 4
 Q = P // B
 SUP_COLS = 256
 NB = 8
-NO = 4
+NST = 6
 
 FLOPS = 2 * B * N * 512 * 768 + 2 * B * F * 2 * N * N + 2 * N * N * B * (F + U)
 BYTES = 2 * (2 * B * F * N + 2 * N * N + 2 * 768 * U + 2 * B * N * U + B * N * 2 * F) + 4 * (
@@ -46,6 +46,11 @@ def tile_gcrnncell_pa_v_kernel(
 
         def bank(name="bank", bufs=NB):
             return psum.tile([P, BANK], F32, name=name, bufs=bufs)
+
+        def stage(own=None):
+            if own:
+                return work.tile([P, WIDE], BF16, name=own, bufs=1, align_bytes=64)
+            return work.tile([P, WIDE], BF16, name="stage", bufs=NST, align_bytes=64)
 
         def quantise(values, fmt, name):
             cols = values.shape[1] // PACK
@@ -77,6 +82,16 @@ def tile_gcrnncell_pa_v_kernel(
                 nc.scalar.copy(out=out, in_=in_)
 
         def interleave(engine, dst, src):
+            if engine == "gpsimd":
+                nc.gpsimd.tensor_scalar(
+                    out=dst.rearrange("p (c t) -> p c t", t=PACK),
+                    in0=src.rearrange("p t c -> p c t"),
+                    scalar1=1.0,
+                    scalar2=0.0,
+                    op0=ALU.mult,
+                    op1=ALU.add,
+                )
+                return
             copy_on(
                 engine,
                 dst.rearrange("p (c i t) -> p c t i", i=RUN, t=PACK),
@@ -131,7 +146,7 @@ def tile_gcrnncell_pa_v_kernel(
             return t
 
         def turn_w_main(w_main):
-            wt = work.tile([P, WIDE], BF16, name="stage", bufs=9, align_bytes=64)
+            wt = stage()
             dst = wt[:].bitcast(F32).rearrange("k (p a u) -> k p a u", a=PACK, u=2)
             for a0 in (0, 2):
                 t = transpose_w(w_main, a0)
@@ -139,7 +154,7 @@ def tile_gcrnncell_pa_v_kernel(
             return wt[:]
 
         def turn_w_unit(w_unit):
-            wu = keep.tile([P, 2 * PACK + 1, Q * PACK], BF16, name="w_unit_padded", align_bytes=64)
+            wu = work.tile([P, 2 * PACK + 1, Q * PACK], BF16, name="own_a", bufs=1, align_bytes=64)
             nc.gpsimd.memset(wu[:, 0 : 2 * PACK + 1 : 2, :], 0.0)
             t = transpose_w(w_unit, 0)
             wu_flat = wu[:].rearrange("k s c -> k (s c)")
@@ -151,11 +166,14 @@ def tile_gcrnncell_pa_v_kernel(
 
         dz_rows, dz_q, dh_banks, dh_vals, dh_q, db_q = {}, {}, {}, {}, {}, {}
 
-        def gate_grad(b, g, s):
+        def gate_grad(b, g, s, own=None):
             sig, grad = gate_in[b, g, s]
             if s == 0:
                 dz_rows[b, g] = work.tile([P, PACK, 2, 2, P], BF16, name="dz_rows", bufs=2)
-            part = work.tile([P, PACK, U], F32, name="part", bufs=2)
+            if own:
+                part = work.tile([P, PACK, U], F32, name=own, bufs=1, align_bytes=64)
+            else:
+                part = work.tile([P, PACK, U], F32, name="part", bufs=2)
             nc.vector.scalar_tensor_tensor(
                 out=part[:], in0=sig[:], scalar=1.0, in1=grad[:], op0=ALU.subtract, op1=ALU.mult
             )
@@ -176,9 +194,9 @@ def tile_gcrnncell_pa_v_kernel(
         def gate(b, g, s):
             gate_round(b, g, s, gate_grad(b, g, s))
 
-        def turn_dz(b, g):
+        def turn_dz(b, g, own=None):
             words = dz_rows[b, g][:].rearrange("p j u s w -> p (j u s w)").bitcast(F32)
-            zt = work.tile([P, WIDE], BF16, name="stage", bufs=9, align_bytes=64)
+            zt = stage(own)
             for h in range(2):
                 t = bank()
                 for c in range(PACK):
@@ -215,9 +233,9 @@ def tile_gcrnncell_pa_v_kernel(
         def quantise_dh(g, i):
             dh_q[g, i] = quantise(dh_vals[g, i][:].rearrange("p r b q j -> p (r b q j)"), E5M2, "dh_%d_%d" % (g, i))
 
-        def turn_dh0(g):
+        def turn_dh0(g, own=None):
             words = dh_vals[g, 0][:].rearrange("p r b q j -> p (r b q j)").bitcast(F32)
-            vals = work.tile([P, WIDE], BF16, name="stage", bufs=9, align_bytes=64)
+            vals = stage(own)
             for u in range(2):
                 t = bank()
                 for c in range(PACK):
@@ -228,8 +246,8 @@ def tile_gcrnncell_pa_v_kernel(
                 )
             return vals
 
-        def dst_part(g, w_unit_q):
-            vals = work.tile([P, WIDE], BF16, name="stage", bufs=9, align_bytes=64)
+        def dst_part(g, w_unit_q, own=None):
+            vals = stage(own)
             for j in range(PACK):
                 t = bank()
                 for c in range(PACK):
@@ -247,9 +265,6 @@ def tile_gcrnncell_pa_v_kernel(
             db_q[g, s] = quantise(vals[:], E5M2, "db_%d_%d" % (g, s))
 
         xs_q, sup_q = {}, {}
-
-        def stage():
-            return work.tile([P, WIDE], BF16, name="stage", bufs=9, align_bytes=64)
 
         def xs_weave(vals, s, h, c, engine):
             interleave(engine, vals[:, c * 1024 : (c + 1) * 1024], rows_in["xs", s][:, :, (2 * h + c) * 256 : (2 * h + c + 1) * 256])
@@ -311,10 +326,9 @@ def tile_gcrnncell_pa_v_kernel(
             for s in range(PACK):
                 out_0_passes(banks[s], slice(0, SUP_COLS), s, quarter, 1)
                 copy_on(("scalar", "vector")[s % 2], res[:, s * SUP_COLS : (s + 1) * SUP_COLS], banks[s][:, :SUP_COLS])
-                if s % 2:
-                    out_0_store(res, quarter, s - 1, s + 1)
+                out_0_store(res, quarter, s, s + 1)
 
-        S, V = "scalar", "vector"
+        S, V, G = "scalar", "vector", "gpsimd"
         load_gate(0, 0, 0)
         load_gate(0, 0, 1)
         load_gate(1, 0, 0)
@@ -343,7 +357,6 @@ def tile_gcrnncell_pa_v_kernel(
         load_gate(1, 1, 1)
         load_grad2(0, 1)
         load_support(0, 1)
-        load_grad2(1, 1)
         quantise_dz(0, 0, z00)
         x00 = stage()
         xs_weave(x00, 0, 0, 0, S)
@@ -357,7 +370,11 @@ def tile_gcrnncell_pa_v_kernel(
         part_010 = gate_grad(0, 1, 0)
         quantise_dz(1, 0, z10)
         gate_round(0, 1, 0, part_010)
+        quantise_xs(0, 0, x00)
         w_unit_q = quantise(wu, E4M3, "w_unit")
+        x11 = stage("own_a")
+        xs_weave(x11, 1, 1, 0, G)
+        xs_weave(x11, 1, 1, 1, G)
         dh_products(0, 0, 0, w_main_q)
         dh_products(1, 0, 0, w_main_q)
         dh_add(0, 0, 0)
@@ -367,85 +384,82 @@ def tile_gcrnncell_pa_v_kernel(
         d0 = dst_part(0, w_unit_q)
         xs_weave(x10, 1, 0, 1, S)
         t0 = turn_dh0(0)
-        x11 = stage()
-        xs_weave(x11, 1, 1, 0, V)
         part_011 = gate_grad(0, 1, 1)
-        quantise_xs(0, 0, x00)
-        gate_round(0, 1, 1, part_011)
         quantise_xs(0, 1, x01)
-        xs_weave(x11, 1, 1, 1, S)
+        gate_round(0, 1, 1, part_011)
         z01 = turn_dz(0, 1)
         load_support(1, 1)
-        s00 = stage()
-        sup_weave(s00, 0, 0, 0, S)
-        s01 = stage()
-        sup_weave(s01, 0, 1, 0, S)
+        load_grad2(1, 1)
+        quantise_xs(1, 1, x11)
         quantise_db(0, 1, d0)
-        part_110 = gate_grad(1, 1, 0)
         quantise_xs(1, 0, x10)
         quantise_db(0, 0, t0)
-        quantise_xs(1, 1, x11)
-        gate_round(1, 1, 0, part_110)
-        quantise_dz(0, 1, z01)
         out_1_part(0, 0, (S, S))
         out_1_part(0, 1, (S, S))
+        part_110 = gate_grad(1, 1, 0)
+        quantise_dz(0, 1, z01)
+        gate_round(1, 1, 0, part_110)
+        out_1_part(0, 2, (S, S))
         dh_products(0, 1, 0, w_main_q)
         dh_products(0, 0, 1, w_main_q)
-        part_111 = gate_grad(1, 1, 1)
-        s02 = stage()
-        sup_weave(s02, 0, 2, 0, S)
+        part_111 = gate_grad(1, 1, 1, "own_b")
+        quantise_dh(0, 0)
         gate_round(1, 1, 1, part_111)
-        z11 = turn_dz(1, 1)
+        s00 = stage("own_b")
+        sup_weave(s00, 0, 0, 0, G)
+        s01 = stage()
+        sup_weave(s01, 0, 1, 0, S)
+        z11 = turn_dz(1, 1, "own_c")
         dh_add(0, 1, 0)
         dh_products(1, 0, 1, w_main_q)
-        dh_add(0, 0, 1)
-        out_1_part(0, 2, (S, S))
         quantise_dz(1, 1, z11)
+        s10 = stage("own_c")
+        sup_weave(s10, 1, 0, 0, G)
+        sup_weave(s10, 1, 0, 1, G)
+        sup_weave(s00, 0, 0, 1, G)
         dh_products(1, 1, 0, w_main_q)
-        dh_add(1, 0, 1)
+        dh_add(0, 0, 1)
         dh_add(1, 1, 0)
-        sup_weave(s00, 0, 0, 1, S)
+        dh_add(1, 0, 1)
+        sup_weave(s01, 0, 1, 1, S)
+        s02 = stage()
+        sup_weave(s02, 0, 2, 0, S)
         d1 = dst_part(1, w_unit_q)
-        t1 = turn_dh0(1)
+        t1 = turn_dh0(1, "own_d")
         dh_products(0, 1, 1, w_main_q)
         dh_products(1, 1, 1, w_main_q)
-        quantise_dh(0, 0)
+        out_1_part(0, 3, (S, S))
         quantise_dh(0, 1)
         quantise_dh(1, 0)
-        quantise_sup(0, 0, s00)
         quantise_db(1, 1, d1)
-        dh_add(0, 1, 1)
+        quantise_sup(1, 0, s10)
         quantise_db(1, 0, t1)
+        s11 = stage("own_d")
+        sup_weave(s11, 1, 1, 0, G)
+        sup_weave(s11, 1, 1, 1, G)
+        dh_add(0, 1, 1)
         dh_add(1, 1, 1)
-        out_1_part(0, 3, (S, S))
-        s10 = stage()
-        sup_weave(s10, 1, 0, 0, V)
-        sup_weave(s10, 1, 0, 1, S)
         out_1_part(1, 0, (S, S))
         out_1_part(1, 1, (S, S))
         quantise_dh(1, 1)
-        quantise_sup(1, 0, s10)
-        sup_weave(s01, 0, 1, 1, V)
-        s11 = stage()
-        sup_weave(s11, 1, 1, 0, V)
+        quantise_sup(0, 0, s00)
+        quantise_sup(0, 1, s01)
         out_1_part(1, 2, (S, S))
         out_1_part(1, 3, (S, S))
-        sup_weave(s11, 1, 1, 1, V)
-        quantise_sup(0, 1, s01)
         sup_weave(s02, 0, 2, 1, V)
         quantise_sup(1, 1, s11)
         s12 = stage()
         sup_weave(s12, 1, 2, 0, V)
         out_0_part(0, (S, S))
-        sup_weave(s12, 1, 2, 1, S)
-        quantise_sup(0, 2, s02)
         s03 = stage()
-        sup_weave(s03, 0, 3, 0, V)
-        quantise_sup(1, 2, s12)
+        sup_weave(s03, 0, 3, 0, S)
+        quantise_sup(0, 2, s02)
+        sup_weave(s12, 1, 2, 1, V)
         sup_weave(s03, 0, 3, 1, V)
+        quantise_sup(1, 2, s12)
         out_0_part(1, (S, S))
         s13 = stage()
-        sup_weave(s13, 1, 3, 0, S)
+        sup_weave(s13, 1, 3, 0, V)
         quantise_sup(0, 3, s03)
         sup_weave(s13, 1, 3, 1, V)
         out_0_part(2, (S, S))

from contextlib import ExitStack

import concourse.mybir as mybir
from concourse.masks import make_identity

B, N, F, U = 2, 1024, 256, 256

F32 = mybir.dt.float32
BF16 = mybir.dt.bfloat16
U32 = mybir.dt.uint32
U8 = mybir.dt.uint8
E4M3 = mybir.dt.float8_e4m3fn_x4
E5M2 = mybir.dt.float8_e5m2_x4
ALU = mybir.AluOpType

P = 128
PACK = 4
K_PASS = P * PACK
HALVES = N // K_PASS
BANK = 512
WIDE = 2048
RUN = 4
Q = P // B
SUP_COLS = 256
NB = 8
NST = 6

FLOPS = 2 * B * N * 512 * 768 + 2 * B * F * 2 * N * N + 2 * N * N * B * (F + U)
BYTES = 2 * (2 * B * F * N + 2 * N * N + 2 * 768 * U + 2 * B * N * U + B * N * 2 * F) + 4 * (
    2 * B * N * U + B * F * N + N * N
)


def tile_gcrnncell_pa_v_kernel(
    tc, inputs, state, support0, support1, r_kernel, u_kernel, r_gate, u_gate, grad_0, grad_1, grad_2, out_0, out_1
):
    nc = tc.nc
    with ExitStack() as ctx:
        keep = ctx.enter_context(tc.tile_pool(name="keep", bufs=1))
        work = ctx.enter_context(tc.tile_pool(name="work", bufs=2))
        psum = ctx.enter_context(tc.psum_pool(name="psum", bufs=8))
        ctx.enter_context(tc.manual_schedule())

        ident = keep.tile([P, P], F32, name="ident")
        make_identity(nc, ident[:])

        def bank(name="bank", bufs=NB):
            return psum.tile([P, BANK], F32, name=name, bufs=bufs)

        def stage(own=None):
            if own:
                return work.tile([P, WIDE], BF16, name=own, bufs=1, align_bytes=64)
            return work.tile([P, WIDE], BF16, name="stage", bufs=NST, align_bytes=64)

        def quantise(values, fmt, name):
            cols = values.shape[1] // PACK
            codes = keep.tile([P, cols], U32, name=name + "_codes", align_bytes=64)
            scales = keep.tile([P, cols], U8, name=name + "_scales", align_bytes=64)
            for c0 in range(0, cols, WIDE // PACK):
                c1 = min(cols, c0 + WIDE // PACK)
                nc.vector.quantize_mx(
                    out=codes[:, c0:c1].bitcast(fmt), scales=scales[:, c0:c1], in_=values[:, PACK * c0 : PACK * c1]
                )
            return codes, scales, fmt

        def product(out, lhs, l0, rhs, r0, start, stop):
            n = out.shape[1]
            nc.tensor.matmul_mx(
                out=out,
                lhsT=lhs[0][:, l0 : l0 + P].bitcast(lhs[2]),
                lhsT_scale=lhs[1][:, l0 : l0 + P],
                rhs=rhs[0][:, r0 : r0 + n].bitcast(rhs[2]),
                rhs_scale=rhs[1][:, r0 : r0 + n],
                start=start,
                stop=stop,
            )

        def copy_on(engine, out, in_):
            if engine == "vector":
                nc.vector.tensor_copy(out=out, in_=in_)
            else:
                nc.scalar.copy(out=out, in_=in_)

        def interleave(engine, dst, src):
            if engine == "gpsimd":
                nc.gpsimd.tensor_scalar(
                    out=dst.rearrange("p (c t) -> p c t", t=PACK),
                    in0=src.rearrange("p t c -> p c t"),
                    scalar1=1.0,
                    scalar2=0.0,
                    op0=ALU.mult,
                    op1=ALU.add,
                )
                return
            copy_on(
                engine,
                dst.rearrange("p (c i t) -> p c t i", i=RUN, t=PACK),
                src.rearrange("p t (c i) -> p c t i", i=RUN),
            )

        def nodes(x, b, g):
            return x[b, g * K_PASS : (g + 1) * K_PASS, :].rearrange("(p j) w -> p j w", j=PACK)

        gate_in, g2_in, rows_in = {}, {}, {}

        def load_gate(b, g, s):
            sig = work.tile([P, PACK, U], F32, name="sig", bufs=4)
            nc.sync.dma_start(out=sig[:], in_=nodes((r_gate, u_gate)[s], b, g))
            grad = work.tile([P, PACK, U], BF16, name="grad", bufs=4)
            nc.sync.dma_start(out=grad[:], in_=nodes((grad_0, grad_1)[s], b, g))
            gate_in[b, g, s] = (sig, grad)

        def load_grad2(b, g):
            t = work.tile([P, PACK, 2 * F], BF16, name="grad2", bufs=4)
            nc.sync.dma_start(out=t[:], in_=nodes(grad_2, b, g))
            g2_in[b, g] = t

        def load_xs(s):
            t = work.tile([P, PACK, N], BF16, name="rows", bufs=4)
            nc.sync.dma_start(out=t[:], in_=(inputs, state)[s].rearrange("b (q t n) -> (b q) t n", t=PACK, n=N))
            rows_in["xs", s] = t

        def load_support(i, g):
            t = work.tile([P, PACK, N], BF16, name="rows", bufs=4)
            src = (support0, support1)[i][g * K_PASS : (g + 1) * K_PASS, :]
            nc.sync.dma_start(out=t[:], in_=src.rearrange("(p j) n -> p j n", j=PACK))
            rows_in["sup", i, g] = t

        def load_w(name, r0, r1):
            a = (r1 - r0) // P
            t = keep.tile([P, a, 2, U], BF16, name=name)
            for s in range(2):
                nc.sync.dma_start(
                    out=t[:, :, s, :], in_=(r_kernel, u_kernel)[s][r0:r1, :].rearrange("(p a) k -> p a k", a=a)
                )
            return t

        def transpose_w(raw, a0):
            words = raw[:].rearrange("p a s k -> p (a s k)").bitcast(F32)
            t = bank()
            for a in range(2):
                for u in range(2):
                    w0 = (a0 + a) * 2 * P
                    c0 = (2 * a + u) * P
                    nc.tensor.transpose(t[:, c0 : c0 + P], words[:, w0 + u : w0 + 2 * P : 2], ident[:])
            return t

        def turn_w_main(w_main):
            wt = stage()
            dst = wt[:].bitcast(F32).rearrange("k (p a u) -> k p a u", a=PACK, u=2)
            for a0 in (0, 2):
                t = transpose_w(w_main, a0)
                nc.scalar.copy(out=dst[:, :, a0 : a0 + 2, :], in_=t[:].rearrange("k (a u p) -> k p a u", a=2, u=2))
            return wt[:]

        def turn_w_unit(w_unit):
            wu = work.tile([P, 2 * PACK + 1, Q * PACK], BF16, name="own_a", bufs=1, align_bytes=64)
            nc.gpsimd.memset(wu[:, 0 : 2 * PACK + 1 : 2, :], 0.0)
            t = transpose_w(w_unit, 0)
            wu_flat = wu[:].rearrange("k s c -> k (s c)")
            sections = wu_flat.bitcast(F32)[:, 2 * Q :].rearrange("k (h a z q u) -> k h a z q u", h=2, a=2, z=2, u=2)
            nc.scalar.copy(
                out=sections[:, :, :, 0, :, :], in_=t[:].rearrange("k (a u q h) -> k h a q u", a=2, u=2, h=2)
            )
            return wu_flat

        dz_rows, dz_q, dh_banks, dh_vals, dh_q, db_q = {}, {}, {}, {}, {}, {}

        def gate_grad(b, g, s, own=None):
            sig, grad = gate_in[b, g, s]
            if s == 0:
                dz_rows[b, g] = work.tile([P, PACK, 2, 2, P], BF16, name="dz_rows", bufs=2)
            if own:
                part = work.tile([P, PACK, U], F32, name=own, bufs=1, align_bytes=64)
            else:
                part = work.tile([P, PACK, U], F32, name="part", bufs=2)
            nc.vector.scalar_tensor_tensor(
                out=part[:], in0=sig[:], scalar=1.0, in1=grad[:], op0=ALU.subtract, op1=ALU.mult
            )
            return part

        def gate_round(b, g, s, part):
            sig = gate_in[b, g, s][0]
            for u in range(2):
                nc.vector.scalar_tensor_tensor(
                    out=dz_rows[b, g][:, :, u, s, :].rearrange("p j (w e) -> p j w e", e=2),
                    in0=part[:].rearrange("p j (w u e) -> p j w u e", u=2, e=2)[:, :, :, u, :],
                    scalar=-1.0,
                    in1=sig[:].rearrange("p j (w u e) -> p j w u e", u=2, e=2)[:, :, :, u, :],
                    op0=ALU.mult,
                    op1=ALU.mult,
                )

        def gate(b, g, s):
            gate_round(b, g, s, gate_grad(b, g, s))

        def turn_dz(b, g, own=None):
            words = dz_rows[b, g][:].rearrange("p j u s w -> p (j u s w)").bitcast(F32)
            zt = stage(own)
            for h in range(2):
                t = bank()
                for c in range(PACK):
                    w0 = (PACK * h + c) * P
                    nc.tensor.transpose(t[:, c * P : (c + 1) * P], words[:, w0 : w0 + P], ident[:])
                nc.scalar.copy(
                    out=zt[:].bitcast(F32)[:, h * BANK : (h + 1) * BANK].rearrange("k (j p u) -> k j p u", j=2, u=2),
                    in_=t[:].rearrange("k (j u p) -> k j p u", j=2, u=2),
                )
            return zt

        def quantise_dz(b, g, zt):
            dz_q[b, g] = quantise(zt[:], E5M2, "dz_%d_%d" % (b, g))

        def dh_products(b, g, i, w_main_q):
            banks = [bank(), bank()]
            for h in range(2):
                for j in range(PACK):
                    product(banks[h][:, j * P : (j + 1) * P], dz_q[b, g], j * P, w_main_q, i * F + h * P, True, True)
            dh_banks[b, g, i] = banks

        def dh_add(b, g, i):
            if b == 0:
                dh_vals[g, i] = work.tile([P, PACK, B, Q, PACK], BF16, name="dh_vals", bufs=4, align_bytes=64)
            for h in range(2):
                c0 = i * F + h * P
                nc.vector.tensor_tensor(
                    out=dh_vals[g, i][:, :, b, h * Q // 2 : (h + 1) * Q // 2, :].rearrange("p r c j -> p c j r"),
                    in0=dh_banks[b, g, i][h][:].rearrange("p (j c r) -> p c j r", j=PACK, r=PACK),
                    in1=g2_in[b, g][:, :, c0 : c0 + P].rearrange("p j (c r) -> p c j r", r=PACK),
                    op=ALU.add,
                )

        def quantise_dh(g, i):
            dh_q[g, i] = quantise(dh_vals[g, i][:].rearrange("p r b q j -> p (r b q j)"), E5M2, "dh_%d_%d" % (g, i))

        def turn_dh0(g, own=None):
            words = dh_vals[g, 0][:].rearrange("p r b q j -> p (r b q j)").bitcast(F32)
            vals = stage(own)
            for u in range(2):
                t = bank()
                for c in range(PACK):
                    nc.tensor.transpose(t[:, c * P : (c + 1) * P], words[:, 2 * c * P + u : 2 * (c + 1) * P : 2], ident[:])
                nc.scalar.copy(
                    out=vals[:, u * 2 * BANK : (u + 1) * 2 * BANK].rearrange("k (e p c) -> k e p c", e=2, c=PACK),
                    in_=t[:].bitcast(BF16).rearrange("k (c p e) -> k e p c", c=PACK, e=2),
                )
            return vals

        def dst_part(g, w_unit_q, own=None):
            vals = stage(own)
            for j in range(PACK):
                t = bank()
                for c in range(PACK):
                    for b in range(B):
                        product(
                            t[:, c * P : (c + 1) * P], w_unit_q, (2 * c + 1 - b) * Q, dz_q[b, g], j * P, b == 0, b == 1
                        )
                nc.scalar.copy(
                    out=vals[:, j * BANK : (j + 1) * BANK].rearrange("k (p c) -> k p c", c=PACK),
                    in_=t[:].rearrange("k (c p) -> k p c", c=PACK),
                )
            return vals

        def quantise_db(g, s, vals):
            db_q[g, s] = quantise(vals[:], E5M2, "db_%d_%d" % (g, s))

        xs_q, sup_q = {}, {}

        def xs_weave(vals, s, h, c, engine):
            interleave(engine, vals[:, c * 1024 : (c + 1) * 1024], rows_in["xs", s][:, :, (2 * h + c) * 256 : (2 * h + c + 1) * 256])

        def quantise_xs(s, h, vals):
            xs_q[s, h] = quantise(vals[:], E4M3, "xs_%d_%d" % (s, h))

        def sup_weave(vals, i, quarter, g, engine):
            c0 = quarter * SUP_COLS
            interleave(
                engine, vals[:, g * 1024 : (g + 1) * 1024], rows_in["sup", i, g][:, :, c0 : c0 + SUP_COLS]
            )

        def quantise_sup(i, quarter, vals):
            sup_q[i, quarter] = quantise(vals[:], E4M3, "sup_%d_%d" % (i, quarter))

        out_1_rows = out_1.rearrange("(g p j) n -> g j p n", p=P, j=PACK)
        out_0_rows = out_0.rearrange("b (q r n) -> (b q) r n", r=PACK, n=N)

        def out_1_part(g, j, engines):
            res = work.tile([P, N], F32, name="res", bufs=5)
            for h in range(2):
                t = bank()
                for s in range(2):
                    product(t[:], db_q[g, s], j * P, xs_q[s, h], 0, s == 0, s == 1)
                copy_on(engines[h], res[:, h * BANK : (h + 1) * BANK], t[:])
            nc.sync.dma_start(out=out_1_rows[g, j], in_=res[:])

        def out_0_passes(t, cols, s, quarter, i):
            for g in range(HALVES):
                product(
                    t[:, cols], dh_q[g, i], s * P, sup_q[i, quarter], g * SUP_COLS, i + g == 0, i + g == HALVES
                )

        def out_0_store(res, quarter, s0, s1):
            nc.sync.dma_start(
                out=out_0_rows[:, s0:s1, quarter * SUP_COLS : (quarter + 1) * SUP_COLS],
                in_=res[:, s0 * SUP_COLS : s1 * SUP_COLS].rearrange("p (s n) -> p s n", n=SUP_COLS),
            )

        def out_0_part(quarter, engines):
            res = work.tile([P, N], F32, name="res", bufs=5)
            for b in range(B):
                t = bank()
                for h in range(2):
                    for i in range(2):
                        out_0_passes(t, slice(h * SUP_COLS, (h + 1) * SUP_COLS), 2 * b + h, quarter, i)
                copy_on(engines[b], res[:, b * BANK : (b + 1) * BANK], t[:])
            out_0_store(res, quarter, 0, PACK)

        def out_0_open(quarter):
            banks = [bank() for s in range(PACK)]
            for s in range(PACK):
                out_0_passes(banks[s], slice(0, SUP_COLS), s, quarter, 0)
            return banks

        def out_0_close(quarter, banks):
            res = work.tile([P, N], F32, name="res", bufs=5)
            for s in range(PACK):
                out_0_passes(banks[s], slice(0, SUP_COLS), s, quarter, 1)
                copy_on(("scalar", "vector")[s % 2], res[:, s * SUP_COLS : (s + 1) * SUP_COLS], banks[s][:, :SUP_COLS])
                out_0_store(res, quarter, s, s + 1)

        S, V, G = "scalar", "vector", "gpsimd"
        load_gate(0, 0, 0)
        load_gate(0, 0, 1)
        load_gate(1, 0, 0)
        w_main = load_w("w_main_rows", 0, 2 * F)
        load_gate(1, 0, 1)
        load_xs(0)
        part_000 = gate_grad(0, 0, 0)
        gate_round(0, 0, 0, part_000)
        load_gate(0, 1, 0)
        w_unit = load_w("w_unit_rows", 2 * F, 2 * F + U)
        load_grad2(0, 0)
        load_xs(1)
        load_grad2(1, 0)
        part_001 = gate_grad(0, 0, 1)
        part_100 = gate_grad(1, 0, 0)
        gate_round(0, 0, 1, part_001)
        load_gate(0, 1, 1)
        wt = turn_w_main(w_main)
        z00 = turn_dz(0, 0)
        gate_round(1, 0, 0, part_100)
        load_gate(1, 1, 0)
        part_101 = gate_grad(1, 0, 1)
        w_main_q = quantise(wt, E4M3, "w_main")
        gate_round(1, 0, 1, part_101)
        load_support(0, 0)
        load_gate(1, 1, 1)
        load_grad2(0, 1)
        load_support(0, 1)
        quantise_dz(0, 0, z00)
        x00 = stage()
        xs_weave(x00, 0, 0, 0, S)
        x01 = stage()
        xs_weave(x01, 0, 1, 0, V)
        z10 = turn_dz(1, 0)
        xs_weave(x00, 0, 0, 1, S)
        wu = turn_w_unit(w_unit)
        xs_weave(x01, 0, 1, 1, S)
        load_support(1, 0)
        part_010 = gate_grad(0, 1, 0)
        quantise_dz(1, 0, z10)
        gate_round(0, 1, 0, part_010)
        quantise_xs(0, 0, x00)
        w_unit_q = quantise(wu, E4M3, "w_unit")
        x11 = stage("own_a")
        xs_weave(x11, 1, 1, 0, G)
        xs_weave(x11, 1, 1, 1, G)
        dh_products(0, 0, 0, w_main_q)
        dh_products(1, 0, 0, w_main_q)
        dh_add(0, 0, 0)
        dh_add(1, 0, 0)
        x10 = stage()
        xs_weave(x10, 1, 0, 0, S)
        d0 = dst_part(0, w_unit_q)
        xs_weave(x10, 1, 0, 1, S)
        t0 = turn_dh0(0)
        part_011 = gate_grad(0, 1, 1)
        quantise_xs(0, 1, x01)
        gate_round(0, 1, 1, part_011)
        z01 = turn_dz(0, 1)
        load_support(1, 1)
        load_grad2(1, 1)
        quantise_xs(1, 1, x11)
        quantise_db(0, 1, d0)
        quantise_xs(1, 0, x10)
        quantise_db(0, 0, t0)
        out_1_part(0, 0, (S, S))
        out_1_part(0, 1, (S, S))
        part_110 = gate_grad(1, 1, 0)
        quantise_dz(0, 1, z01)
        gate_round(1, 1, 0, part_110)
        out_1_part(0, 2, (S, S))
        dh_products(0, 1, 0, w_main_q)
        dh_products(0, 0, 1, w_main_q)
        part_111 = gate_grad(1, 1, 1, "own_b")
        quantise_dh(0, 0)
        gate_round(1, 1, 1, part_111)
        s00 = stage("own_b")
        sup_weave(s00, 0, 0, 0, G)
        s01 = stage()
        sup_weave(s01, 0, 1, 0, S)
        z11 = turn_dz(1, 1, "own_c")
        dh_add(0, 1, 0)
        dh_products(1, 0, 1, w_main_q)
        quantise_dz(1, 1, z11)
        s10 = stage("own_c")
        sup_weave(s10, 1, 0, 0, G)
        sup_weave(s10, 1, 0, 1, G)
        sup_weave(s00, 0, 0, 1, G)
        dh_products(1, 1, 0, w_main_q)
        dh_add(0, 0, 1)
        dh_add(1, 1, 0)
        dh_add(1, 0, 1)
        sup_weave(s01, 0, 1, 1, S)
        s02 = stage()
        sup_weave(s02, 0, 2, 0, S)
        d1 = dst_part(1, w_unit_q)
        t1 = turn_dh0(1, "own_d")
        dh_products(0, 1, 1, w_main_q)
        dh_products(1, 1, 1, w_main_q)
        out_1_part(0, 3, (S, S))
        quantise_dh(0, 1)
        quantise_dh(1, 0)
        quantise_db(1, 1, d1)
        quantise_sup(1, 0, s10)
        quantise_db(1, 0, t1)
        s11 = stage("own_d")
        sup_weave(s11, 1, 1, 0, G)
        sup_weave(s11, 1, 1, 1, G)
        dh_add(0, 1, 1)
        dh_add(1, 1, 1)
        out_1_part(1, 0, (S, S))
        out_1_part(1, 1, (S, S))
        quantise_dh(1, 1)
        quantise_sup(0, 0, s00)
        quantise_sup(0, 1, s01)
        out_1_part(1, 2, (S, S))
        out_1_part(1, 3, (S, S))
        sup_weave(s02, 0, 2, 1, V)
        quantise_sup(1, 1, s11)
        s12 = stage()
        sup_weave(s12, 1, 2, 0, V)
        out_0_part(0, (S, S))
        s03 = stage()
        sup_weave(s03, 0, 3, 0, S)
        quantise_sup(0, 2, s02)
        sup_weave(s12, 1, 2, 1, V)
        sup_weave(s03, 0, 3, 1, V)
        quantise_sup(1, 2, s12)
        out_0_part(1, (S, S))
        s13 = stage()
        sup_weave(s13, 1, 3, 0, V)
        quantise_sup(0, 3, s03)
        sup_weave(s13, 1, 3, 1, V)
        out_0_part(2, (S, S))
        quantise_sup(1, 3, s13)
        last = out_0_open(3)
        out_0_close(3, last)
